import numpy as np
import ml_dtypes


def mxq(x, axis, fmt="e4m3"):
    dtype, down = {"e4m3": (ml_dtypes.float8_e4m3fn, 7), "e5m2": (ml_dtypes.float8_e5m2, 14)}[fmt]
    v = np.moveaxis(np.asarray(x, np.float32).astype(ml_dtypes.bfloat16).astype(np.float64), axis, -1)
    blocks = v.reshape(v.shape[:-1] + (-1, 32))
    amax = np.abs(blocks).max(-1, keepdims=True)
    byte = np.maximum(np.where(amax > 0, np.frexp(amax)[1] - 1 + 127, 0) - down, 1)
    scale = np.exp2(byte - 127.0)
    codes = (blocks / scale).astype(np.float32).astype(dtype).astype(np.float64)
    return np.moveaxis((codes * scale).reshape(v.shape), -1, axis)


WIDE = False


def mx_kscale(k):
    if not WIDE:
        return np.ones(k)
    levels = np.array([30, -30])
    if k % 512:
        return np.exp2(np.random.permutation(np.resize(levels, k // 32))).repeat(32)
    a = np.empty((k // 512, 16))
    for p in range(k // 512):
        a[p, :8] = np.random.permutation(np.resize(levels, 8))
        for g in range(8):
            far = levels[np.abs(levels - a[p, g]) >= 10]
            a[p, g + 8] = far[np.random.randint(len(far))]
    return np.exp2(a.ravel()).repeat(32)


BF16 = ml_dtypes.bfloat16


def bf(x):
    return np.asarray(x, np.float32).astype(BF16)


def f64(x):
    return np.asarray(x).astype(np.float64)


B, S, HIDDEN, H, HKV, D = 1, 512, 2048, 16, 4, 128
THETA = 10000.0
QS, KVS = H * D, HKV * D
HALF = D // 2


def rope(x):
    freqs = 1.0 / THETA ** (np.arange(0, D, 2) / D)
    ang = np.arange(S)[:, None] * freqs[None, :]
    cos = np.cos(ang)[None, :, None, :]
    sin = np.sin(ang)[None, :, None, :]
    x1, x2 = x[..., :HALF], x[..., HALF:]
    return np.concatenate([x1 * cos - x2 * sin, x1 * sin + x2 * cos], axis=-1)


def setup_inputs():
    s = mx_kscale(HIDDEN)
    return {"hidden_states": bf(np.random.standard_normal((B, S, HIDDEN)) * s),
            "w_qkv": bf(np.random.standard_normal((QS + 2 * KVS, HIDDEN)) * 1.2 / np.sqrt(HIDDEN) / s)}


def reference(hidden_states, w_qkv):
    qkv = mxq(f64(hidden_states), 2, "e5m2") @ mxq(f64(w_qkv), 1, "e5m2").T
    xq = qkv[..., :QS].reshape(B, S, H, D)
    xk = qkv[..., QS:QS + KVS].reshape(B, S, HKV, D)
    xv = qkv[..., QS + KVS:].reshape(B, S, HKV, D)
    return rope(xq), rope(xk), xv

@@ -1,0 +1,256 @@
+from contextlib import ExitStack
+
+import concourse.mybir as mybir
+from concourse.masks import make_identity
+
+FLOPS = 2 * 512 * 3072 * 2048
+
+F32 = mybir.dt.float32
+BF16 = mybir.dt.bfloat16
+U32 = mybir.dt.uint32
+U8 = mybir.dt.uint8
+I32 = mybir.dt.int32
+E5X4 = mybir.dt.float8_e5m2_x4
+ALU = mybir.AluOpType
+ACTF = mybir.ActivationFunctionType
+
+P = 128
+K = 2048
+PASSES = 4
+THETA = 10000.0
+PI = 3.141592653589793
+PI_1 = 3.140625
+PI_2 = int((PI - PI_1) * 4194304.0) / 4194304.0
+PI_3 = PI - PI_1 - PI_2
+N_UNITS = 28
+RAW_BUFS = 20
+
+
+def freq(i):
+    return 1.0 / THETA ** (i / 64.0)
+
+
+def tile_gemmaattention_pa_kernel(tc, hidden_states, w_qkv, out_0, out_1, out_2):
+    nc = tc.nc
+    x2d = hidden_states.rearrange("b s k -> (b s) k")
+    q2d = out_0.rearrange("b s h d -> (b s) (h d)")
+    k2d = out_1.rearrange("b s h d -> (b s) (h d)")
+    v2d = out_2.rearrange("b s h d -> (b s) (h d)")
+
+    def out_block(n, t):
+        rows = slice(P * t, P * (t + 1))
+        if n < 4:
+            return q2d[rows, 512 * n : 512 * (n + 1)]
+        if n == 4:
+            return k2d[rows, :]
+        return v2d[rows, :]
+
+    def unit_info(u):
+        if u < 4:
+            return ("w", 0, u)
+        if u < 8:
+            return ("x", (u - 4) // 2, (u - 4) % 2)
+        return ("w", (u - 4) // 4, (u - 4) % 4)
+
+    def unit_rows(u):
+        kind, grp_i, pos = unit_info(u)
+        if kind == "x":
+            r0 = P * (2 * grp_i + pos)
+            return x2d[r0 : r0 + P, :]
+        r0 = 512 * grp_i + P * pos
+        return w_qkv[r0 : r0 + P, :]
+
+    with ExitStack() as ctx:
+        const = ctx.enter_context(tc.tile_pool(name="const", bufs=1))
+        rawp = ctx.enter_context(tc.tile_pool(name="rawp", bufs=RAW_BUFS))
+        grpp = ctx.enter_context(tc.tile_pool(name="grpp", bufs=2))
+        codp = ctx.enter_context(tc.tile_pool(name="codp", bufs=3))
+        prodp = ctx.enter_context(tc.tile_pool(name="prodp", bufs=4))
+        yp = ctx.enter_context(tc.tile_pool(name="yp", bufs=8))
+        ps_t = ctx.enter_context(tc.psum_pool(name="ps_t", bufs=4))
+        ps_a = ctx.enter_context(tc.psum_pool(name="ps_a", bufs=4))
+        ctx.enter_context(tc.manual_schedule())
+
+        raws = {}
+
+        def load(u):
+            r = rawp.tile([P, K], BF16, name="raw", tag="raw")
+            nc.sync.dma_start(out=r[:], in_=unit_rows(u))
+            raws[u] = r
+
+        for u in range(RAW_BUFS):
+            load(u)
+
+        pos_i = const.tile([P, 4], I32, name="pos_i")
+        nc.gpsimd.iota(pos_i[:], pattern=[[P, 4]], base=0, channel_multiplier=1)
+        ident = const.tile([P, P], F32, name="ident")
+        make_identity(nc, ident[:])
+
+        one = const.tile([P, 1], F32, name="one")
+        nc.vector.memset(one[:], 1.0)
+        junk = const.tile([P, 1], F32, name="junk")
+        nc.scalar.activation(out=junk[:], in_=one[:], func=ACTF.Sin)
+
+        pos_f = const.tile([P, 4], F32, name="pos_f")
+        nc.vector.tensor_copy(out=pos_f[:], in_=pos_i[:])
+        f_lo = const.tile([P, 8], F32, name="f_lo")
+        for b in range(8):
+            nc.vector.tensor_scalar_mul(out=f_lo[:, b : b + 1], in0=one[:, 0:1], scalar1=freq(b))
+        freqs = const.tile([P, 64], F32, name="freqs")
+        for a in range(8):
+            nc.vector.tensor_scalar_mul(out=freqs[:, 8 * a : 8 * a + 8], in0=f_lo[:], scalar1=freq(8 * a))
+        ang = const.tile([P, 256], F32, name="ang")
+        for t in range(4):
+            nc.vector.tensor_scalar_mul(out=ang[:, 64 * t : 64 * t + 64], in0=freqs[:], scalar1=pos_f[:, t : t + 1])
+        n_i = const.tile([P, 256], I32, name="n_i")
+        nc.vector.tensor_single_scalar(out=n_i[:], in_=ang[:], scalar=1.0 / PI, op=ALU.mult)
+        n_f = const.tile([P, 256], F32, name="n_f")
+        nc.vector.tensor_copy(out=n_f[:], in_=n_i[:])
+        red1 = const.tile([P, 256], F32, name="red1")
+        nc.vector.scalar_tensor_tensor(out=red1[:], in0=n_f[:], scalar=-PI_1, in1=ang[:], op0=ALU.mult, op1=ALU.add)
+        red2 = const.tile([P, 256], F32, name="red2")
+        nc.vector.scalar_tensor_tensor(out=red2[:], in0=n_f[:], scalar=-PI_2, in1=red1[:], op0=ALU.mult, op1=ALU.add)
+        red3 = const.tile([P, 256], F32, name="red3")
+        nc.vector.scalar_tensor_tensor(out=red3[:], in0=n_f[:], scalar=-PI_3, in1=red2[:], op0=ALU.mult, op1=ALU.add)
+        sin_r = const.tile([P, 256], F32, name="sin_r")
+        nc.scalar.activation(out=sin_r[:], in_=red3[:], func=ACTF.Sin)
+        sin_h = const.tile([P, 256], F32, name="sin_h")
+        nc.scalar.activation(out=sin_h[:], in_=red3[:], func=ACTF.Sin, scale=0.5)
+        par_i = const.tile([P, 256], I32, name="par_i")
+        nc.vector.tensor_single_scalar(out=par_i[:], in_=n_i[:], scalar=1, op=ALU.bitwise_and)
+        sgn = const.tile([P, 256], F32, name="sgn")
+        nc.vector.tensor_scalar(out=sgn[:], in0=par_i[:], scalar1=-2.0, scalar2=1.0, op0=ALU.mult, op1=ALU.add)
+        nsgn = const.tile([P, 256], F32, name="nsgn")
+        nc.vector.tensor_scalar(out=nsgn[:], in0=par_i[:], scalar1=2.0, scalar2=-1.0, op0=ALU.mult, op1=ALU.add)
+        hh = const.tile([P, 256], F32, name="hh")
+        nc.vector.tensor_tensor(out=hh[:], in0=sin_h[:], in1=sin_h[:], op=ALU.mult)
+        cos_r = const.tile([P, 256], F32, name="cos_r")
+        nc.vector.tensor_scalar(out=cos_r[:], in0=hh[:], scalar1=-2.0, scalar2=1.0, op0=ALU.mult, op1=ALU.add)
+        tab = const.tile([P, 4, 4, 64], F32, name="tab")
+
+        def by_t(tile_ap):
+            return tile_ap[:].rearrange("p (t i) -> p t i", t=4)
+
+        nc.vector.tensor_tensor(out=tab[:, :, 0, :], in0=by_t(sgn), in1=by_t(cos_r), op=ALU.mult)
+        nc.vector.tensor_tensor(out=tab[:, :, 1, :], in0=by_t(sgn), in1=by_t(sin_r), op=ALU.mult)
+        nc.vector.tensor_tensor(out=tab[:, :, 2, :], in0=by_t(nsgn), in1=by_t(sin_r), op=ALU.mult)
+        nc.vector.tensor_tensor(out=tab[:, :, 3, :], in0=by_t(sgn), in1=by_t(cos_r), op=ALU.mult)
+
+        grouped = {}
+        codes = {}
+
+        def transpose_unit(u):
+            kind, grp_i, pos = unit_info(u)
+            ncols = 256 if kind == "x" else 512
+            if pos == 0:
+                grouped[(kind, grp_i)] = grpp.tile(
+                    [P, PASSES, ncols, 4], BF16, name="grp_" + kind, tag="grp_" + kind, align_bytes=64
+                )
+            g32 = grouped[(kind, grp_i)][:].bitcast(F32)
+            words = raws[u][:].bitcast(F32)
+            rope_order = kind == "w" and grp_i < 5
+            for b in range(2):
+                bank = ps_t.tile([P, 512], F32, name="tp", tag="tp")
+                for gg in range(2):
+                    g = 2 * b + gg
+                    for uu in range(2):
+                        s = 2 * gg + uu
+                        nc.tensor.transpose(
+                            bank[:, P * s : P * (s + 1)], words[:, 256 * g + uu : 256 * (g + 1) : 2], ident[:]
+                        )
+                if rope_order:
+                    dst = g32.rearrange("p g (two h i) u -> p g two h i u", two=2, h=4)[:, 2 * b : 2 * b + 2, :, pos, :, :]
+                    src = bank[:].rearrange("p (g u two i) -> p g two i u", g=2, u=2, two=2)
+                else:
+                    dst = g32[:, 2 * b : 2 * b + 2, P * pos : P * (pos + 1), :]
+                    src = bank[:].rearrange("p (g u r) -> p g r u", g=2, u=2)
+                nc.scalar.copy(out=dst, in_=src)
+
+        def quantize_group(kind, grp_i):
+            ncols = 256 if kind == "x" else 512
+            bufs = 2 if kind == "x" else 3
+            c = codp.tile([P, PASSES, ncols], U32, name="cod_" + kind, tag="cod_" + kind, bufs=bufs, align_bytes=64)
+            s = codp.tile([P, PASSES, ncols], U8, name="scl_" + kind, tag="scl_" + kind, bufs=bufs, align_bytes=64)
+            codes[(kind, grp_i)] = (c, s)
+            g = grouped[(kind, grp_i)]
+            step = 4096 // (4 * ncols)
+            for lo in range(0, PASSES, step):
+                nc.vector.quantize_mx(
+                    out=c[:, lo : lo + step, :].rearrange("p g c -> p (g c)").bitcast(E5X4),
+                    scales=s[:, lo : lo + step, :].rearrange("p g c -> p (g c)"),
+                    in_=g[:, lo : lo + step, :, :].rearrange("p g c t -> p (g c t)"),
+                )
+
+        def t2(k):
+            for u in (2 * k, 2 * k + 1):
+                transpose_unit(u)
+                if u + RAW_BUFS < N_UNITS:
+                    load(u + RAW_BUFS)
+                kind, grp_i, pos = unit_info(u)
+                if pos == (1 if kind == "x" else 3):
+                    quantize_group(kind, grp_i)
+
+        def mx(n, t):
+            acc = ps_a.tile([P, 512], F32, name="acc", tag="acc")
+            xc, xs = codes[("x", t // 2)]
+            wc, ws = codes[("w", n)]
+            cols = slice(P * (t % 2), P * (t % 2) + P)
+            for g in range(PASSES):
+                nc.tensor.matmul_mx(
+                    out=acc[:],
+                    lhsT=xc[:, g, cols].bitcast(E5X4),
+                    lhsT_scale=xs[:, g, cols],
+                    rhs=wc[:, g, :].bitcast(E5X4),
+                    rhs_scale=ws[:, g, :],
+                    start=(g == 0),
+                    stop=(g == PASSES - 1),
+                )
+            return acc
+
+        def rope_mul(acc, t):
+            pr = prodp.tile([P, 4, 256], F32, name="pr", tag="pr")
+            nc.vector.tensor_tensor(
+                out=pr[:].rearrange("p (two j) (h i) -> p two j h i", two=2, h=4),
+                in0=acc[:].rearrange("p (two o h i) -> p two o h i", two=2, o=1, h=4).to_broadcast([P, 2, 2, 4, 64]),
+                in1=tab[:, t, :, :].rearrange("p (two j) (o i) -> p two j o i", two=2, o=1).to_broadcast([P, 2, 2, 4, 64]),
+                op=ALU.mult,
+            )
+            return pr
+
+        def rope_add(pr, n, t):
+            y = yp.tile([P, 512], F32, name="y", tag="y")
+            nc.vector.tensor_tensor(
+                out=y[:].rearrange("p (h two i) -> p two h i", two=2, i=64),
+                in0=pr[:, 0:2, :].rearrange("p two (h i) -> p two h i", h=4),
+                in1=pr[:, 2:4, :].rearrange("p two (h i) -> p two h i", h=4),
+                op=ALU.add,
+            )
+            nc.sync.dma_start(out=out_block(n, t), in_=y[:])
+
+        def mx_rope(n, ts):
+            accs = [mx(n, t) for t in ts]
+            if n < 5:
+                prs = [rope_mul(acc, t) for acc, t in zip(accs, ts)]
+                for pr, t in zip(prs, ts):
+                    rope_add(pr, n, t)
+            else:
+                for acc, t in zip(accs, ts):
+                    y = yp.tile([P, 512], F32, name="y", tag="y")
+                    nc.scalar.copy(out=y[:], in_=acc[:])
+                    nc.sync.dma_start(out=out_block(n, t), in_=y[:])
+
+        for k in range(4):
+            t2(k)
+        mx_rope(0, [0, 1])
+        t2(4)
+        mx_rope(0, [2])
+        t2(5)
+        mx_rope(0, [3])
+        t2(6)
+        k = 7
+        for n in range(1, 6):
+            for ts in ([0, 1], [2, 3]):
+                mx_rope(n, ts)
+                if k < N_UNITS // 2:
+                    t2(k)
+                    k += 1

@@ -24,6 +24,9 @@ PI_2 = int((PI - PI_1) * 4194304.0) / 4194304.0
 PI_3 = PI - PI_1 - PI_2
 N_UNITS = 28
 RAW_BUFS = 20
+WARM_FIRST = 6
+WARM_UNITS = 7
+WARM_PER_UNIT = 2
 
 
 def freq(i):
@@ -73,6 +76,13 @@ def tile_gemmaattention_pa_kernel(tc, hidden_states, w_qkv, out_0, out_1, out_2)
 
         raws = {}
 
+        zeros = const.tile([P, 512], BF16, name="zeros")
+
+        def warm(count):
+            scratch = ps_a.tile([P, 512], F32, name="acc", tag="acc")
+            for i in range(count):
+                nc.tensor.matmul(scratch[:], lhsT=zeros[:, 0:P], rhs=zeros[:], start=True, stop=True)
+
         def load(u):
             r = rawp.tile([P, K], BF16, name="raw", tag="raw")
             nc.sync.dma_start(out=r[:], in_=unit_rows(u))
@@ -83,6 +93,7 @@ def tile_gemmaattention_pa_kernel(tc, hidden_states, w_qkv, out_0, out_1, out_2)
 
         pos_i = const.tile([P, 4], I32, name="pos_i")
         nc.gpsimd.iota(pos_i[:], pattern=[[P, 4]], base=0, channel_multiplier=1)
+        nc.gpsimd.memset(zeros[:], 0.0)
         ident = const.tile([P, P], F32, name="ident")
         make_identity(nc, ident[:])
 
@@ -184,6 +195,8 @@ def tile_gemmaattention_pa_kernel(tc, hidden_states, w_qkv, out_0, out_1, out_2)
         def t2(k):
             for u in (2 * k, 2 * k + 1):
                 transpose_unit(u)
+                if u < WARM_UNITS:
+                    warm(WARM_PER_UNIT)
                 if u + RAW_BUFS < N_UNITS:
                     load(u + RAW_BUFS)
                 kind, grp_i, pos = unit_info(u)
@@ -239,6 +252,7 @@ def tile_gemmaattention_pa_kernel(tc, hidden_states, w_qkv, out_0, out_1, out_2)
                     nc.scalar.copy(out=y[:], in_=acc[:])
                     nc.sync.dma_start(out=out_block(n, t), in_=y[:])
 
+        warm(WARM_FIRST)
         for k in range(4):
             t2(k)
         mx_rope(0, [0, 1])

@@ -23,10 +23,9 @@ PI_1 = 3.140625
 PI_2 = int((PI - PI_1) * 4194304.0) / 4194304.0
 PI_3 = PI - PI_1 - PI_2
 N_UNITS = 28
-RAW_BUFS = 20
-WARM_FIRST = 6
-WARM_UNITS = 7
-WARM_PER_UNIT = 2
+RAW_BUFS = 12
+V_REORDERED = (1, 2, 3, 4, 5)
+S_REORDER_AFTER = {3: 9, 4: 11, 5: 13, 6: 15, 7: 17, 8: 19, 9: 21, 10: 23, 11: 25, 12: 27}
 
 
 def freq(i):
@@ -69,19 +68,13 @@ def tile_gemmaattention_pa_kernel(tc, hidden_states, w_qkv, out_0, out_1, out_2)
         grpp = ctx.enter_context(tc.tile_pool(name="grpp", bufs=2))
         codp = ctx.enter_context(tc.tile_pool(name="codp", bufs=3))
         prodp = ctx.enter_context(tc.tile_pool(name="prodp", bufs=4))
-        yp = ctx.enter_context(tc.tile_pool(name="yp", bufs=8))
+        yp = ctx.enter_context(tc.tile_pool(name="yp", bufs=12))
+        rep = ctx.enter_context(tc.tile_pool(name="rep", bufs=8))
         ps_t = ctx.enter_context(tc.psum_pool(name="ps_t", bufs=4))
         ps_a = ctx.enter_context(tc.psum_pool(name="ps_a", bufs=4))
         ctx.enter_context(tc.manual_schedule())
 
         raws = {}
-
-        zeros = const.tile([P, 512], BF16, name="zeros")
-
-        def warm(count):
-            scratch = ps_a.tile([P, 512], F32, name="acc", tag="acc")
-            for i in range(count):
-                nc.tensor.matmul(scratch[:], lhsT=zeros[:, 0:P], rhs=zeros[:], start=True, stop=True)
 
         def load(u):
             r = rawp.tile([P, K], BF16, name="raw", tag="raw")
@@ -91,9 +84,15 @@ def tile_gemmaattention_pa_kernel(tc, hidden_states, w_qkv, out_0, out_1, out_2)
         for u in range(RAW_BUFS):
             load(u)
 
+        reord = {}
+
+        def reorder(u, copy_fn):
+            re = rep.tile([P, PASSES, 2, P], F32, name="re", tag="re")
+            copy_fn(out=re[:], in_=raws[u][:].bitcast(F32).rearrange("p (g w u) -> p g u w", g=PASSES, u=2))
+            reord[u] = re
+
         pos_i = const.tile([P, 4], I32, name="pos_i")
         nc.gpsimd.iota(pos_i[:], pattern=[[P, 4]], base=0, channel_multiplier=1)
-        nc.gpsimd.memset(zeros[:], 0.0)
         ident = const.tile([P, P], F32, name="ident")
         make_identity(nc, ident[:])
 
@@ -128,24 +127,34 @@ def tile_gemmaattention_pa_kernel(tc, hidden_states, w_qkv, out_0, out_1, out_2)
         sin_h = const.tile([P, 256], F32, name="sin_h")
         nc.scalar.activation(out=sin_h[:], in_=red3[:], func=ACTF.Sin, scale=0.5)
         par_i = const.tile([P, 256], I32, name="par_i")
-        nc.vector.tensor_single_scalar(out=par_i[:], in_=n_i[:], scalar=1, op=ALU.bitwise_and)
         sgn = const.tile([P, 256], F32, name="sgn")
-        nc.vector.tensor_scalar(out=sgn[:], in0=par_i[:], scalar1=-2.0, scalar2=1.0, op0=ALU.mult, op1=ALU.add)
         nsgn = const.tile([P, 256], F32, name="nsgn")
-        nc.vector.tensor_scalar(out=nsgn[:], in0=par_i[:], scalar1=2.0, scalar2=-1.0, op0=ALU.mult, op1=ALU.add)
         hh = const.tile([P, 256], F32, name="hh")
-        nc.vector.tensor_tensor(out=hh[:], in0=sin_h[:], in1=sin_h[:], op=ALU.mult)
         cos_r = const.tile([P, 256], F32, name="cos_r")
-        nc.vector.tensor_scalar(out=cos_r[:], in0=hh[:], scalar1=-2.0, scalar2=1.0, op0=ALU.mult, op1=ALU.add)
         tab = const.tile([P, 4, 4, 64], F32, name="tab")
 
         def by_t(tile_ap):
             return tile_ap[:].rearrange("p (t i) -> p t i", t=4)
 
-        nc.vector.tensor_tensor(out=tab[:, :, 0, :], in0=by_t(sgn), in1=by_t(cos_r), op=ALU.mult)
-        nc.vector.tensor_tensor(out=tab[:, :, 1, :], in0=by_t(sgn), in1=by_t(sin_r), op=ALU.mult)
-        nc.vector.tensor_tensor(out=tab[:, :, 2, :], in0=by_t(nsgn), in1=by_t(sin_r), op=ALU.mult)
-        nc.vector.tensor_tensor(out=tab[:, :, 3, :], in0=by_t(sgn), in1=by_t(cos_r), op=ALU.mult)
+        def table_step(j):
+            if j == 0:
+                nc.vector.tensor_single_scalar(out=par_i[:], in_=n_i[:], scalar=1, op=ALU.bitwise_and)
+                nc.vector.tensor_scalar(out=sgn[:], in0=par_i[:], scalar1=-2.0, scalar2=1.0, op0=ALU.mult, op1=ALU.add)
+            elif j == 1:
+                nc.vector.tensor_scalar(out=nsgn[:], in0=par_i[:], scalar1=2.0, scalar2=-1.0, op0=ALU.mult, op1=ALU.add)
+                nc.vector.tensor_tensor(out=hh[:], in0=sin_h[:], in1=sin_h[:], op=ALU.mult)
+            elif j == 2:
+                nc.vector.tensor_scalar(out=cos_r[:], in0=hh[:], scalar1=-2.0, scalar2=1.0, op0=ALU.mult, op1=ALU.add)
+                nc.vector.tensor_tensor(out=tab[:, :, 1, :], in0=by_t(sgn), in1=by_t(sin_r), op=ALU.mult)
+            elif j == 3:
+                nc.vector.tensor_tensor(out=tab[:, :, 2, :], in0=by_t(nsgn), in1=by_t(sin_r), op=ALU.mult)
+                nc.vector.tensor_tensor(out=tab[:, :, 0, :], in0=by_t(sgn), in1=by_t(cos_r), op=ALU.mult)
+            elif j == 4:
+                nc.vector.tensor_tensor(out=tab[:, :, 3, :], in0=by_t(sgn), in1=by_t(cos_r), op=ALU.mult)
+
+        for j, u in enumerate(V_REORDERED):
+            reorder(u, nc.vector.tensor_copy)
+            table_step(j)
 
         grouped = {}
         codes = {}
@@ -166,9 +175,11 @@ def tile_gemmaattention_pa_kernel(tc, hidden_states, w_qkv, out_0, out_1, out_2)
                     g = 2 * b + gg
                     for uu in range(2):
                         s = 2 * gg + uu
-                        nc.tensor.transpose(
-                            bank[:, P * s : P * (s + 1)], words[:, 256 * g + uu : 256 * (g + 1) : 2], ident[:]
-                        )
+                        if u in reord:
+                            t_in = reord[u][:, g, uu, :]
+                        else:
+                            t_in = words[:, 256 * g + uu : 256 * (g + 1) : 2]
+                        nc.tensor.transpose(bank[:, P * s : P * (s + 1)], t_in, ident[:])
                 if rope_order:
                     dst = g32.rearrange("p g (two h i) u -> p g two h i u", two=2, h=4)[:, 2 * b : 2 * b + 2, :, pos, :, :]
                     src = bank[:].rearrange("p (g u two i) -> p g two i u", g=2, u=2, two=2)
@@ -195,13 +206,13 @@ def tile_gemmaattention_pa_kernel(tc, hidden_states, w_qkv, out_0, out_1, out_2)
         def t2(k):
             for u in (2 * k, 2 * k + 1):
                 transpose_unit(u)
-                if u < WARM_UNITS:
-                    warm(WARM_PER_UNIT)
                 if u + RAW_BUFS < N_UNITS:
                     load(u + RAW_BUFS)
                 kind, grp_i, pos = unit_info(u)
                 if pos == (1 if kind == "x" else 3):
                     quantize_group(kind, grp_i)
+            if k in S_REORDER_AFTER:
+                reorder(S_REORDER_AFTER[k], nc.scalar.copy)
 
         def mx(n, t):
             acc = ps_a.tile([P, 512], F32, name="acc", tag="acc")
@@ -232,7 +243,8 @@ def tile_gemmaattention_pa_kernel(tc, hidden_states, w_qkv, out_0, out_1, out_2)
 
         def rope_add(pr, n, t):
             y = yp.tile([P, 512], F32, name="y", tag="y")
-            nc.vector.tensor_tensor(
+            add_engine = nc.gpsimd if t % 2 == 0 else nc.vector
+            add_engine.tensor_tensor(
                 out=y[:].rearrange("p (h two i) -> p two h i", two=2, i=64),
                 in0=pr[:, 0:2, :].rearrange("p two (h i) -> p two h i", h=4),
                 in1=pr[:, 2:4, :].rearrange("p two (h i) -> p two h i", h=4),
@@ -252,7 +264,6 @@ def tile_gemmaattention_pa_kernel(tc, hidden_states, w_qkv, out_0, out_1, out_2)
                     nc.scalar.copy(out=y[:], in_=acc[:])
                     nc.sync.dma_start(out=out_block(n, t), in_=y[:])
 
-        warm(WARM_FIRST)
         for k in range(4):
             t2(k)
         mx_rope(0, [0, 1])

@@ -243,8 +243,7 @@ def tile_gemmaattention_pa_kernel(tc, hidden_states, w_qkv, out_0, out_1, out_2)
 
         def rope_add(pr, n, t):
             y = yp.tile([P, 512], F32, name="y", tag="y")
-            add_engine = nc.gpsimd if t % 2 == 0 else nc.vector
-            add_engine.tensor_tensor(
+            nc.gpsimd.tensor_tensor(
                 out=y[:].rearrange("p (h two i) -> p two h i", two=2, i=64),
                 in0=pr[:, 0:2, :].rearrange("p two (h i) -> p two h i", h=4),
                 in1=pr[:, 2:4, :].rearrange("p two (h i) -> p two h i", h=4),

@@ -24,7 +24,7 @@ PI_2 = int((PI - PI_1) * 4194304.0) / 4194304.0
 PI_3 = PI - PI_1 - PI_2
 N_UNITS = 28
 RAW_BUFS = 12
-V_REORDERED = (1, 2, 3, 4, 5)
+V_REORDERED = ()
 S_REORDER_AFTER = {3: 9, 4: 11, 5: 13, 6: 15, 7: 17, 8: 19, 9: 21, 10: 23, 11: 25, 12: 27}
 
 
@@ -152,8 +152,7 @@ def tile_gemmaattention_pa_kernel(tc, hidden_states, w_qkv, out_0, out_1, out_2)
             elif j == 4:
                 nc.vector.tensor_tensor(out=tab[:, :, 3, :], in0=by_t(sgn), in1=by_t(cos_r), op=ALU.mult)
 
-        for j, u in enumerate(V_REORDERED):
-            reorder(u, nc.vector.tensor_copy)
+        for j in range(5):
             table_step(j)
 
         grouped = {}

@@ -25,7 +25,7 @@ PI_3 = PI - PI_1 - PI_2
 N_UNITS = 28
 RAW_BUFS = 12
 V_REORDERED = ()
-S_REORDER_AFTER = {3: 9, 4: 11, 5: 13, 6: 15, 7: 17, 8: 19, 9: 21, 10: 23, 11: 25, 12: 27}
+S_REORDER_AFTER = {4: 11, 5: 13, 6: 15, 7: 17, 8: 19, 9: 21, 10: 23, 11: 25, 12: 27}
 
 
 def freq(i):
@@ -214,7 +214,10 @@ def tile_gemmaattention_pa_kernel(tc, hidden_states, w_qkv, out_0, out_1, out_2)
                 reorder(S_REORDER_AFTER[k], nc.scalar.copy)
 
         def mx(n, t):
-            acc = ps_a.tile([P, 512], F32, name="acc", tag="acc")
+            if n == 5:
+                acc = ps_t.tile([P, 512], F32, name="tp", tag="tp")
+            else:
+                acc = ps_a.tile([P, 512], F32, name="acc", tag="acc")
             xc, xs = codes[("x", t // 2)]
             wc, ws = codes[("w", n)]
             cols = slice(P * (t % 2), P * (t % 2) + P)
@@ -242,7 +245,8 @@ def tile_gemmaattention_pa_kernel(tc, hidden_states, w_qkv, out_0, out_1, out_2)
 
         def rope_add(pr, n, t):
             y = yp.tile([P, 512], F32, name="y", tag="y")
-            nc.gpsimd.tensor_tensor(
+            add_engine = nc.vector if (n, t) == (4, 3) else nc.gpsimd
+            add_engine.tensor_tensor(
                 out=y[:].rearrange("p (h two i) -> p two h i", two=2, i=64),
                 in0=pr[:, 0:2, :].rearrange("p two (h i) -> p two h i", h=4),
                 in1=pr[:, 2:4, :].rearrange("p two (h i) -> p two h i", h=4),
@@ -260,17 +264,17 @@ def tile_gemmaattention_pa_kernel(tc, hidden_states, w_qkv, out_0, out_1, out_2)
                 for acc, t in zip(accs, ts):
                     y = yp.tile([P, 512], F32, name="y", tag="y")
                     nc.scalar.copy(out=y[:], in_=acc[:])
-                    nc.sync.dma_start(out=out_block(n, t), in_=y[:])
+                    nc.scalar.dma_start(out=out_block(n, t), in_=y[:])
 
-        for k in range(4):
+        for k in range(5):
             t2(k)
         mx_rope(0, [0, 1])
-        t2(4)
-        mx_rope(0, [2])
         t2(5)
-        mx_rope(0, [3])
+        mx_rope(0, [2])
         t2(6)
-        k = 7
+        mx_rope(0, [3])
+        t2(7)
+        k = 8
         for n in range(1, 6):
             for ts in ([0, 1], [2, 3]):
                 mx_rope(n, ts)

@@ -25,7 +25,6 @@ PI_3 = PI - PI_1 - PI_2
 N_UNITS = 28
 RAW_BUFS = 12
 V_REORDERED = ()
-S_REORDER_AFTER = {4: 11, 5: 13, 6: 15, 7: 17, 8: 19, 9: 21, 10: 23, 11: 25, 12: 27}
 
 
 def freq(i):
@@ -202,16 +201,15 @@ def tile_gemmaattention_pa_kernel(tc, hidden_states, w_qkv, out_0, out_1, out_2)
                     in_=g[:, lo : lo + step, :, :].rearrange("p g c t -> p (g c t)"),
                 )
 
-        def t2(k):
-            for u in (2 * k, 2 * k + 1):
-                transpose_unit(u)
-                if u + RAW_BUFS < N_UNITS:
-                    load(u + RAW_BUFS)
-                kind, grp_i, pos = unit_info(u)
-                if pos == (1 if kind == "x" else 3):
-                    quantize_group(kind, grp_i)
-            if k in S_REORDER_AFTER:
-                reorder(S_REORDER_AFTER[k], nc.scalar.copy)
+        def t1(u):
+            transpose_unit(u)
+            if u + RAW_BUFS < N_UNITS:
+                load(u + RAW_BUFS)
+            kind, grp_i, pos = unit_info(u)
+            if pos == (1 if kind == "x" else 3):
+                quantize_group(kind, grp_i)
+            if u % 2 == 1 and 11 <= u + 2 < N_UNITS:
+                reorder(u + 2, nc.scalar.copy)
 
         def mx(n, t):
             if n == 5:
@@ -266,18 +264,17 @@ def tile_gemmaattention_pa_kernel(tc, hidden_states, w_qkv, out_0, out_1, out_2)
                     nc.scalar.copy(out=y[:], in_=acc[:])
                     nc.scalar.dma_start(out=out_block(n, t), in_=y[:])
 
-        for k in range(5):
-            t2(k)
-        mx_rope(0, [0, 1])
-        t2(5)
-        mx_rope(0, [2])
-        t2(6)
-        mx_rope(0, [3])
-        t2(7)
-        k = 8
-        for n in range(1, 6):
+        for u in range(10):
+            t1(u)
+        for step in ((0, 0), 10, (0, 1), 11, 12, (0, 2), 13, 14, (0, 3), 15):
+            if isinstance(step, int):
+                t1(step)
+            else:
+                mx_rope(step[0], [step[1]])
+        for n in range(1, 4):
+            for t in range(4):
+                mx_rope(n, [t])
+                t1(12 + 4 * n + t)
+        for n in (4, 5):
             for ts in ([0, 1], [2, 3]):
                 mx_rope(n, ts)
-                if k < N_UNITS // 2:
-                    t2(k)
-                    k += 1

@@ -189,8 +189,8 @@ def tile_gemmaattention_pa_kernel(tc, hidden_states, w_qkv, out_0, out_1, out_2)
         def quantize_group(kind, grp_i):
             ncols = 256 if kind == "x" else 512
             bufs = 2 if kind == "x" else 3
-            c = codp.tile([P, PASSES, ncols], U32, name="cod_" + kind, tag="cod_" + kind, bufs=bufs, align_bytes=64)
-            s = codp.tile([P, PASSES, ncols], U8, name="scl_" + kind, tag="scl_" + kind, bufs=bufs, align_bytes=64)
+            c = codp.tile([P, PASSES, ncols], U32, name="cod_" + kind, tag="cod_" + kind, bufs=bufs, align_bytes=256)
+            s = codp.tile([P, PASSES, ncols], U8, name="scl_" + kind, tag="scl_" + kind, bufs=bufs, align_bytes=256)
             codes[(kind, grp_i)] = (c, s)
             g = grouped[(kind, grp_i)]
             step = 4096 // (4 * ncols)

@@ -24,7 +24,7 @@ PI_2 = int((PI - PI_1) * 4194304.0) / 4194304.0
 PI_3 = PI - PI_1 - PI_2
 N_UNITS = 28
 RAW_BUFS = 12
-V_REORDERED = ()
+V_COPIES = (0, 1, 2, 3)
 
 
 def freq(i):
@@ -122,9 +122,14 @@ def tile_gemmaattention_pa_kernel(tc, hidden_states, w_qkv, out_0, out_1, out_2)
         red3 = const.tile([P, 256], F32, name="red3")
         nc.vector.scalar_tensor_tensor(out=red3[:], in0=n_f[:], scalar=-PI_3, in1=red2[:], op0=ALU.mult, op1=ALU.add)
         sin_r = const.tile([P, 256], F32, name="sin_r")
-        nc.scalar.activation(out=sin_r[:], in_=red3[:], func=ACTF.Sin)
         sin_h = const.tile([P, 256], F32, name="sin_h")
-        nc.scalar.activation(out=sin_h[:], in_=red3[:], func=ACTF.Sin, scale=0.5)
+
+        def sine_step(j):
+            if j == 0:
+                nc.scalar.activation(out=sin_h[:], in_=red3[:], func=ACTF.Sin, scale=0.5)
+            elif j == 1:
+                nc.scalar.activation(out=sin_r[:], in_=red3[:], func=ACTF.Sin)
+
         par_i = const.tile([P, 256], I32, name="par_i")
         sgn = const.tile([P, 256], F32, name="sgn")
         nsgn = const.tile([P, 256], F32, name="nsgn")
@@ -150,9 +155,6 @@ def tile_gemmaattention_pa_kernel(tc, hidden_states, w_qkv, out_0, out_1, out_2)
                 nc.vector.tensor_tensor(out=tab[:, :, 0, :], in0=by_t(sgn), in1=by_t(cos_r), op=ALU.mult)
             elif j == 4:
                 nc.vector.tensor_tensor(out=tab[:, :, 3, :], in0=by_t(sgn), in1=by_t(cos_r), op=ALU.mult)
-
-        for j in range(5):
-            table_step(j)
 
         grouped = {}
         codes = {}
@@ -184,7 +186,16 @@ def tile_gemmaattention_pa_kernel(tc, hidden_states, w_qkv, out_0, out_1, out_2)
                 else:
                     dst = g32[:, 2 * b : 2 * b + 2, P * pos : P * (pos + 1), :]
                     src = bank[:].rearrange("p (g u r) -> p g r u", g=2, u=2)
-                nc.scalar.copy(out=dst, in_=src)
+                if u in V_COPIES and b == 1:
+                    nc.vector.tensor_copy(out=dst, in_=src)
+                else:
+                    nc.scalar.copy(out=dst, in_=src)
+                if b == 0 and u < 2:
+                    sine_step(u)
+            if u < 4:
+                table_step(u)
+            if u == 3:
+                table_step(4)
 
         def quantize_group(kind, grp_i):
             ncols = 256 if kind == "x" else 512

@@ -219,7 +219,7 @@ def tile_gemmaattention_pa_kernel(tc, hidden_states, w_qkv, out_0, out_1, out_2)
             kind, grp_i, pos = unit_info(u)
             if pos == (1 if kind == "x" else 3):
                 quantize_group(kind, grp_i)
-            if u % 2 == 1 and 11 <= u + 2 < N_UNITS:
+            if u % 2 == 1 and 13 <= u + 2 < N_UNITS:
                 reorder(u + 2, nc.scalar.copy)
 
         def mx(n, t):
@@ -275,14 +275,9 @@ def tile_gemmaattention_pa_kernel(tc, hidden_states, w_qkv, out_0, out_1, out_2)
                     nc.scalar.copy(out=y[:], in_=acc[:])
                     nc.scalar.dma_start(out=out_block(n, t), in_=y[:])
 
-        for u in range(10):
+        for u in range(12):
             t1(u)
-        for step in ((0, 0), 10, (0, 1), 11, 12, (0, 2), 13, 14, (0, 3), 15):
-            if isinstance(step, int):
-                t1(step)
-            else:
-                mx_rope(step[0], [step[1]])
-        for n in range(1, 4):
+        for n in range(4):
             for t in range(4):
                 mx_rope(n, [t])
                 t1(12 + 4 * n + t)

from contextlib import ExitStack

import concourse.mybir as mybir
from concourse.masks import make_identity

FLOPS = 2 * 512 * 3072 * 2048

F32 = mybir.dt.float32
BF16 = mybir.dt.bfloat16
U32 = mybir.dt.uint32
U8 = mybir.dt.uint8
I32 = mybir.dt.int32
E5X4 = mybir.dt.float8_e5m2_x4
ALU = mybir.AluOpType
ACTF = mybir.ActivationFunctionType

P = 128
K = 2048
PASSES = 4
THETA = 10000.0
PI = 3.141592653589793
PI_1 = 3.140625
PI_2 = int((PI - PI_1) * 4194304.0) / 4194304.0
PI_3 = PI - PI_1 - PI_2
N_UNITS = 28
RAW_BUFS = 12
V_COPIES = (0, 1, 2, 3)


def freq(i):
    return 1.0 / THETA ** (i / 64.0)


def tile_gemmaattention_pa_kernel(tc, hidden_states, w_qkv, out_0, out_1, out_2):
    nc = tc.nc
    x2d = hidden_states.rearrange("b s k -> (b s) k")
    q2d = out_0.rearrange("b s h d -> (b s) (h d)")
    k2d = out_1.rearrange("b s h d -> (b s) (h d)")
    v2d = out_2.rearrange("b s h d -> (b s) (h d)")

    def out_block(n, t):
        rows = slice(P * t, P * (t + 1))
        if n < 4:
            return q2d[rows, 512 * n : 512 * (n + 1)]
        if n == 4:
            return k2d[rows, :]
        return v2d[rows, :]

    def unit_info(u):
        if u < 4:
            return ("w", 0, u)
        if u < 8:
            return ("x", (u - 4) // 2, (u - 4) % 2)
        return ("w", (u - 4) // 4, (u - 4) % 4)

    def unit_rows(u):
        kind, grp_i, pos = unit_info(u)
        if kind == "x":
            r0 = P * (2 * grp_i + pos)
            return x2d[r0 : r0 + P, :]
        r0 = 512 * grp_i + P * pos
        return w_qkv[r0 : r0 + P, :]

    with ExitStack() as ctx:
        const = ctx.enter_context(tc.tile_pool(name="const", bufs=1))
        rawp = ctx.enter_context(tc.tile_pool(name="rawp", bufs=RAW_BUFS))
        grpp = ctx.enter_context(tc.tile_pool(name="grpp", bufs=2))
        codp = ctx.enter_context(tc.tile_pool(name="codp", bufs=3))
        prodp = ctx.enter_context(tc.tile_pool(name="prodp", bufs=4))
        yp = ctx.enter_context(tc.tile_pool(name="yp", bufs=12))
        rep = ctx.enter_context(tc.tile_pool(name="rep", bufs=8))
        ps_t = ctx.enter_context(tc.psum_pool(name="ps_t", bufs=4))
        ps_a = ctx.enter_context(tc.psum_pool(name="ps_a", bufs=4))
        ctx.enter_context(tc.manual_schedule())

        raws = {}

        def load(u):
            r = rawp.tile([P, K], BF16, name="raw", tag="raw")
            nc.sync.dma_start(out=r[:], in_=unit_rows(u))
            raws[u] = r

        for u in range(RAW_BUFS):
            load(u)

        reord = {}

        def reorder(u, copy_fn):
            re = rep.tile([P, PASSES, 2, P], F32, name="re", tag="re")
            copy_fn(out=re[:], in_=raws[u][:].bitcast(F32).rearrange("p (g w u) -> p g u w", g=PASSES, u=2))
            reord[u] = re

        pos_i = const.tile([P, 4], I32, name="pos_i")
        nc.gpsimd.iota(pos_i[:], pattern=[[P, 4]], base=0, channel_multiplier=1)
        ident = const.tile([P, P], F32, name="ident")
        make_identity(nc, ident[:])

        one = const.tile([P, 1], F32, name="one")
        nc.vector.memset(one[:], 1.0)
        junk = const.tile([P, 1], F32, name="junk")
        nc.scalar.activation(out=junk[:], in_=one[:], func=ACTF.Sin)

        pos_f = const.tile([P, 4], F32, name="pos_f")
        nc.vector.tensor_copy(out=pos_f[:], in_=pos_i[:])
        f_lo = const.tile([P, 8], F32, name="f_lo")
        for b in range(8):
            nc.vector.tensor_scalar_mul(out=f_lo[:, b : b + 1], in0=one[:, 0:1], scalar1=freq(b))
        freqs = const.tile([P, 64], F32, name="freqs")
        for a in range(8):
            nc.vector.tensor_scalar_mul(out=freqs[:, 8 * a : 8 * a + 8], in0=f_lo[:], scalar1=freq(8 * a))
        ang = const.tile([P, 256], F32, name="ang")
        for t in range(4):
            nc.vector.tensor_scalar_mul(out=ang[:, 64 * t : 64 * t + 64], in0=freqs[:], scalar1=pos_f[:, t : t + 1])
        n_i = const.tile([P, 256], I32, name="n_i")
        nc.vector.tensor_single_scalar(out=n_i[:], in_=ang[:], scalar=1.0 / PI, op=ALU.mult)
        n_f = const.tile([P, 256], F32, name="n_f")
        nc.vector.tensor_copy(out=n_f[:], in_=n_i[:])
        red1 = const.tile([P, 256], F32, name="red1")
        nc.vector.scalar_tensor_tensor(out=red1[:], in0=n_f[:], scalar=-PI_1, in1=ang[:], op0=ALU.mult, op1=ALU.add)
        red2 = const.tile([P, 256], F32, name="red2")
        nc.vector.scalar_tensor_tensor(out=red2[:], in0=n_f[:], scalar=-PI_2, in1=red1[:], op0=ALU.mult, op1=ALU.add)
        red3 = const.tile([P, 256], F32, name="red3")
        nc.vector.scalar_tensor_tensor(out=red3[:], in0=n_f[:], scalar=-PI_3, in1=red2[:], op0=ALU.mult, op1=ALU.add)
        sin_r = const.tile([P, 256], F32, name="sin_r")
        sin_h = const.tile([P, 256], F32, name="sin_h")

        def sine_step(j):
            if j == 0:
                nc.scalar.activation(out=sin_h[:], in_=red3[:], func=ACTF.Sin, scale=0.5)
            elif j == 1:
                nc.scalar.activation(out=sin_r[:], in_=red3[:], func=ACTF.Sin)

        par_i = const.tile([P, 256], I32, name="par_i")
        sgn = const.tile([P, 256], F32, name="sgn")
        nsgn = const.tile([P, 256], F32, name="nsgn")
        hh = const.tile([P, 256], F32, name="hh")
        cos_r = const.tile([P, 256], F32, name="cos_r")
        tab = const.tile([P, 4, 4, 64], F32, name="tab")

        def by_t(tile_ap):
            return tile_ap[:].rearrange("p (t i) -> p t i", t=4)

        def table_step(j):
            if j == 0:
                nc.vector.tensor_single_scalar(out=par_i[:], in_=n_i[:], scalar=1, op=ALU.bitwise_and)
                nc.vector.tensor_scalar(out=sgn[:], in0=par_i[:], scalar1=-2.0, scalar2=1.0, op0=ALU.mult, op1=ALU.add)
            elif j == 1:
                nc.vector.tensor_scalar(out=nsgn[:], in0=par_i[:], scalar1=2.0, scalar2=-1.0, op0=ALU.mult, op1=ALU.add)
                nc.vector.tensor_tensor(out=hh[:], in0=sin_h[:], in1=sin_h[:], op=ALU.mult)
            elif j == 2:
                nc.vector.tensor_scalar(out=cos_r[:], in0=hh[:], scalar1=-2.0, scalar2=1.0, op0=ALU.mult, op1=ALU.add)
                nc.vector.tensor_tensor(out=tab[:, :, 1, :], in0=by_t(sgn), in1=by_t(sin_r), op=ALU.mult)
            elif j == 3:
                nc.vector.tensor_tensor(out=tab[:, :, 2, :], in0=by_t(nsgn), in1=by_t(sin_r), op=ALU.mult)
                nc.vector.tensor_tensor(out=tab[:, :, 0, :], in0=by_t(sgn), in1=by_t(cos_r), op=ALU.mult)
            elif j == 4:
                nc.vector.tensor_tensor(out=tab[:, :, 3, :], in0=by_t(sgn), in1=by_t(cos_r), op=ALU.mult)

        grouped = {}
        codes = {}

        def transpose_unit(u):
            kind, grp_i, pos = unit_info(u)
            ncols = 256 if kind == "x" else 512
            if pos == 0:
                grouped[(kind, grp_i)] = grpp.tile(
                    [P, PASSES, ncols, 4], BF16, name="grp_" + kind, tag="grp_" + kind, align_bytes=64
                )
            g32 = grouped[(kind, grp_i)][:].bitcast(F32)
            words = raws[u][:].bitcast(F32)
            rope_order = kind == "w" and grp_i < 5
            for b in range(2):
                bank = ps_t.tile([P, 512], F32, name="tp", tag="tp")
                for gg in range(2):
                    g = 2 * b + gg
                    for uu in range(2):
                        s = 2 * gg + uu
                        if u in reord:
                            t_in = reord[u][:, g, uu, :]
                        else:
                            t_in = words[:, 256 * g + uu : 256 * (g + 1) : 2]
                        nc.tensor.transpose(bank[:, P * s : P * (s + 1)], t_in, ident[:])
                if rope_order:
                    dst = g32.rearrange("p g (two h i) u -> p g two h i u", two=2, h=4)[:, 2 * b : 2 * b + 2, :, pos, :, :]
                    src = bank[:].rearrange("p (g u two i) -> p g two i u", g=2, u=2, two=2)
                else:
                    dst = g32[:, 2 * b : 2 * b + 2, P * pos : P * (pos + 1), :]
                    src = bank[:].rearrange("p (g u r) -> p g r u", g=2, u=2)
                if u in V_COPIES and b == 1:
                    nc.vector.tensor_copy(out=dst, in_=src)
                else:
                    nc.scalar.copy(out=dst, in_=src)
                if b == 0 and u < 2:
                    sine_step(u)
            if u < 4:
                table_step(u)
            if u == 3:
                table_step(4)

        def quantize_group(kind, grp_i):
            ncols = 256 if kind == "x" else 512
            bufs = 2 if kind == "x" else 3
            c = codp.tile([P, PASSES, ncols], U32, name="cod_" + kind, tag="cod_" + kind, bufs=bufs, align_bytes=256)
            s = codp.tile([P, PASSES, ncols], U8, name="scl_" + kind, tag="scl_" + kind, bufs=bufs, align_bytes=256)
            codes[(kind, grp_i)] = (c, s)
            g = grouped[(kind, grp_i)]
            step = 4096 // (4 * ncols)
            for lo in range(0, PASSES, step):
                nc.vector.quantize_mx(
                    out=c[:, lo : lo + step, :].rearrange("p g c -> p (g c)").bitcast(E5X4),
                    scales=s[:, lo : lo + step, :].rearrange("p g c -> p (g c)"),
                    in_=g[:, lo : lo + step, :, :].rearrange("p g c t -> p (g c t)"),
                )

        def t1(u):
            transpose_unit(u)
            if u + RAW_BUFS < N_UNITS:
                load(u + RAW_BUFS)
            kind, grp_i, pos = unit_info(u)
            if pos == (1 if kind == "x" else 3):
                quantize_group(kind, grp_i)
            if u % 2 == 1 and 13 <= u + 2 < N_UNITS:
                reorder(u + 2, nc.scalar.copy)

        def mx(n, t):
            if n == 5:
                acc = ps_t.tile([P, 512], F32, name="tp", tag="tp")
            else:
                acc = ps_a.tile([P, 512], F32, name="acc", tag="acc")
            xc, xs = codes[("x", t // 2)]
            wc, ws = codes[("w", n)]
            cols = slice(P * (t % 2), P * (t % 2) + P)
            for g in range(PASSES):
                nc.tensor.matmul_mx(
                    out=acc[:],
                    lhsT=xc[:, g, cols].bitcast(E5X4),
                    lhsT_scale=xs[:, g, cols],
                    rhs=wc[:, g, :].bitcast(E5X4),
                    rhs_scale=ws[:, g, :],
                    start=(g == 0),
                    stop=(g == PASSES - 1),
                )
            return acc

        def rope_mul(acc, t):
            pr = prodp.tile([P, 4, 256], F32, name="pr", tag="pr")
            nc.vector.tensor_tensor(
                out=pr[:].rearrange("p (two j) (h i) -> p two j h i", two=2, h=4),
                in0=acc[:].rearrange("p (two o h i) -> p two o h i", two=2, o=1, h=4).to_broadcast([P, 2, 2, 4, 64]),
                in1=tab[:, t, :, :].rearrange("p (two j) (o i) -> p two j o i", two=2, o=1).to_broadcast([P, 2, 2, 4, 64]),
                op=ALU.mult,
            )
            return pr

        def rope_add(pr, n, t):
            y = yp.tile([P, 512], F32, name="y", tag="y")
            add_engine = nc.vector if (n, t) == (4, 3) else nc.gpsimd
            add_engine.tensor_tensor(
                out=y[:].rearrange("p (h two i) -> p two h i", two=2, i=64),
                in0=pr[:, 0:2, :].rearrange("p two (h i) -> p two h i", h=4),
                in1=pr[:, 2:4, :].rearrange("p two (h i) -> p two h i", h=4),
                op=ALU.add,
            )
            nc.sync.dma_start(out=out_block(n, t), in_=y[:])

        def mx_rope(n, ts):
            accs = [mx(n, t) for t in ts]
            if n < 5:
                prs = [rope_mul(acc, t) for acc, t in zip(accs, ts)]
                for pr, t in zip(prs, ts):
                    rope_add(pr, n, t)
            else:
                for acc, t in zip(accs, ts):
                    y = yp.tile([P, 512], F32, name="y", tag="y")
                    nc.scalar.copy(out=y[:], in_=acc[:])
                    nc.scalar.dma_start(out=out_block(n, t), in_=y[:])

        for u in range(12):
            t1(u)
        for n in range(4):
            for t in range(4):
                mx_rope(n, [t])
                t1(12 + 4 * n + t)
        for n in (4, 5):
            for ts in ([0, 1], [2, 3]):
                mx_rope(n, ts)
